import numpy as np
import ml_dtypes


def mxq(x, axis, fmt="e4m3"):
    dtype, down = {"e4m3": (ml_dtypes.float8_e4m3fn, 7), "e5m2": (ml_dtypes.float8_e5m2, 14)}[fmt]
    v = np.moveaxis(np.asarray(x, np.float32).astype(ml_dtypes.bfloat16).astype(np.float64), axis, -1)
    blocks = v.reshape(v.shape[:-1] + (-1, 32))
    amax = np.abs(blocks).max(-1, keepdims=True)
    byte = np.maximum(np.where(amax > 0, np.frexp(amax)[1] - 1 + 127, 0) - down, 1)
    scale = np.exp2(byte - 127.0)
    codes = (blocks / scale).astype(np.float32).astype(dtype).astype(np.float64)
    return np.moveaxis((codes * scale).reshape(v.shape), -1, axis)


WIDE = False


def mx_kscale(k):
    if not WIDE:
        return np.ones(k)
    levels = np.array([20, -20, 10, -10, 0])
    a = np.random.permutation(np.resize(levels, k // 512 * 4)).reshape(k // 512, 4)
    idx = np.arange(k)
    return np.exp2(a[idx // 512, idx % 128 // 32])


BF16 = ml_dtypes.bfloat16


def bf(x):
    return np.asarray(x, np.float32).astype(BF16)


def f64(x):
    return np.asarray(x).astype(np.float64)


B, S, K, N = 4, 256, 1024, 2560
T = B * S


def setup_inputs():
    s = mx_kscale(T).reshape(B, S, 1)
    x = np.random.standard_normal((B, S, K)) * s
    weight = np.random.standard_normal((N, K)) * (1.0 / np.sqrt(K))
    wscales = np.random.uniform(0.5, 1.5, (N, 1))
    bias = np.random.standard_normal((1, N)) * 0.3
    g = np.random.standard_normal((B, S, N)) * np.exp2(np.random.randint(-12, 1, (B, S, 1))) / s
    return {"x": bf(x), "weight": bf(weight), "wscales": bf(wscales), "bias": bf(bias), "grad_out": bf(g)}


def reference(x, weight, wscales, bias, grad_out):
    x2 = f64(x).reshape(-1, weight.shape[1])
    g2 = f64(grad_out).reshape(-1, weight.shape[0])
    dwd = mxq(g2, 0, "e5m2").T @ mxq(x2, 0, "e4m3")
    return dwd * f64(wscales)

@@ -1,0 +1,164 @@
+from contextlib import ExitStack
+
+import concourse.mybir as mybir
+
+T_TOKENS, K_FEAT, N_FEAT = 1024, 1024, 2560
+FLOPS = 2 * T_TOKENS * K_FEAT * N_FEAT
+BYTES = 2 * (T_TOKENS * K_FEAT + T_TOKENS * N_FEAT + N_FEAT) + 4 * N_FEAT * K_FEAT
+
+BF16 = mybir.dt.bfloat16
+F32 = mybir.dt.float32
+U32 = mybir.dt.uint32
+U8 = mybir.dt.uint8
+E4M3 = mybir.dt.float8_e4m3fn_x4
+E5M2 = mybir.dt.float8_e5m2_x4
+COPY = mybir.ActivationFunctionType.Copy
+MULT = mybir.AluOpType.mult
+
+P = 128
+PACK = 4
+PASSES = T_TOKENS // (P * PACK)
+N_TILE = 512
+HALVES = K_FEAT // N_TILE
+TILES = 4
+GROUPS = N_FEAT // (TILES * P)
+UNIT = PACK * N_TILE
+RUN = 4
+CHUNKS = ((0, 2), (2, 5))
+VECTOR_GROUPS = (0, 3, 4)
+
+
+def tile_unicorelinearfp4_kernel(tc, x, weight, wscales, bias, grad_out, out):
+    nc = tc.nc
+    x_rows = x.flatten_outer_dims().rearrange("(c p j) k -> c p j k", c=PASSES, p=P, j=PACK)
+    g_rows = grad_out.flatten_outer_dims().rearrange("(c p j) n -> c p j n", c=PASSES, p=P, j=PACK)
+    out_rows = out.rearrange("(g p i) k -> g p i k", p=P, i=TILES)
+    ws_cols = wscales.rearrange("(g p i) o -> p g (i o)", p=P, i=TILES)
+
+    with ExitStack() as ctx:
+        raw = ctx.enter_context(tc.tile_pool(name="raw", bufs=1))
+        stage = ctx.enter_context(tc.tile_pool(name="stage", bufs=6))
+        keep = ctx.enter_context(tc.tile_pool(name="keep", bufs=1))
+        res = ctx.enter_context(tc.tile_pool(name="res", bufs=1))
+        psum = ctx.enter_context(tc.psum_pool(name="psum", bufs=8))
+        ctx.enter_context(tc.manual_schedule())
+
+        x_raw = {}
+        g_raw = {}
+        x_q = {}
+        g_q = {}
+        acc = {}
+
+        def load_x(c):
+            x_raw[c] = raw.tile([P, PACK, K_FEAT], BF16, name="x_raw%d" % c)
+            nc.sync.dma_start(out=x_raw[c][:], in_=x_rows[c, :, :, :])
+
+        def load_g(chunk, c):
+            g0, g1 = CHUNKS[chunk]
+            width = (g1 - g0) * N_TILE
+            g_raw[(chunk, c)] = raw.tile([P, PACK, width], BF16, name="g_raw%d_%d" % (chunk, c))
+            nc.sync.dma_start(
+                out=g_raw[(chunk, c)][:], in_=g_rows[c, :, :, g0 * N_TILE : g1 * N_TILE]
+            )
+
+        def regroup_x(copy, c, h):
+            grouped = stage.tile([P, UNIT], BF16, name="grouped", align_bytes=64)
+            copy(
+                out=grouped[:].rearrange("p (w i j) -> p w j i", i=RUN, j=PACK),
+                in_=x_raw[c][:, :, h * N_TILE : (h + 1) * N_TILE].rearrange(
+                    "p j (w i) -> p w j i", i=RUN
+                ),
+            )
+            return grouped
+
+        def regroup_g(copy, c, g):
+            chunk = [n for n, (g0, g1) in enumerate(CHUNKS) if g0 <= g < g1][0]
+            first = (g - CHUNKS[chunk][0]) * N_TILE
+            grouped = stage.tile([P, UNIT], BF16, name="grouped", align_bytes=64)
+            copy(
+                out=grouped[:].rearrange("p (i w j) -> p w j i", i=TILES, j=PACK),
+                in_=g_raw[(chunk, c)][:, :, first : first + N_TILE].rearrange(
+                    "p j (w i) -> p w j i", i=TILES
+                ),
+            )
+            return grouped
+
+        def quantise(grouped, fmt, name):
+            codes = keep.tile([P, N_TILE], U32, name=name + "_codes", align_bytes=64)
+            scales = keep.tile([P, N_TILE], U8, name=name + "_scales", align_bytes=64)
+            nc.vector.quantize_mx(out=codes[:].bitcast(fmt), scales=scales[:], in_=grouped[:])
+            return codes, scales
+
+        def multiply(t, c):
+            g, i = divmod(t, TILES)
+            codes, scales = g_q[(c, g)]
+            cols = slice(i * P, (i + 1) * P)
+            for h in range(HALVES):
+                if c == 0:
+                    acc[(t, h)] = psum.tile([P, N_TILE], F32, name="acc")
+                x_codes, x_scales = x_q[(c, h)]
+                nc.tensor.matmul_mx(
+                    out=acc[(t, h)][:],
+                    lhsT=codes[:, cols].bitcast(E5M2),
+                    lhsT_scale=scales[:, cols],
+                    rhs=x_codes[:].bitcast(E4M3),
+                    rhs_scale=x_scales[:],
+                    start=(c == 0),
+                    stop=(c == PASSES - 1),
+                )
+
+        def empty(t, h, on_vector):
+            g, i = divmod(t, TILES)
+            dst = result[g][:, i, h * N_TILE : (h + 1) * N_TILE]
+            if on_vector:
+                nc.vector.tensor_scalar(
+                    out=dst, in0=acc[(t, h)][:], scalar1=ws[:, t : t + 1], scalar2=None, op0=MULT
+                )
+            else:
+                nc.scalar.activation(out=dst, in_=acc[(t, h)][:], func=COPY, scale=ws[:, t : t + 1])
+
+        load_x(0)
+        load_g(0, 0)
+        load_x(1)
+        load_g(0, 1)
+        load_g(1, 0)
+        load_g(1, 1)
+
+        ws_bf = keep.tile([P, GROUPS, TILES], BF16, name="ws_bf")
+        ws = keep.tile([P, GROUPS * TILES], F32, name="ws")
+        with nc.allow_non_contiguous_dma(reason="wscales: 4 neighbouring rows of out a partition"):
+            nc.scalar.dma_start(out=ws_bf[:], in_=ws_cols)
+        nc.scalar.activation(out=ws[:], in_=ws_bf[:].rearrange("p g i -> p (g i)"), func=COPY)
+
+        result = [res.tile([P, TILES, K_FEAT], F32, name="result%d" % g) for g in range(GROUPS)]
+
+        later = {}
+        for c in range(PASSES):
+            first = regroup_x(nc.vector.tensor_copy, c, 0)
+            second = regroup_x(nc.scalar.copy, c, 1)
+            x_q[(c, 0)] = quantise(first, E4M3, "x%d_0" % c)
+            x_q[(c, 1)] = quantise(second, E4M3, "x%d_1" % c)
+            first = regroup_g(nc.vector.tensor_copy, c, 0)
+            later[c] = regroup_g(nc.scalar.copy, c, 1)
+            g_q[(c, 0)] = quantise(first, E5M2, "g%d_0" % c)
+            for t in range(TILES):
+                multiply(t, c)
+        for c in range(PASSES):
+            g_q[(c, 1)] = quantise(later[c], E5M2, "g%d_1" % c)
+
+        for t in range(GROUPS * TILES):
+            if t == TILES:
+                for g in range(2, GROUPS):
+                    pair = [regroup_g(nc.vector.tensor_copy, c, g) for c in range(PASSES)]
+                    for c in range(PASSES):
+                        g_q[(c, g)] = quantise(pair[c], E5M2, "g%d_%d" % (c, g))
+            empty(t, 0, False)
+            empty(t, 1, t // TILES in VECTOR_GROUPS)
+            if t % 2 == 1:
+                g, i = divmod(t, TILES)
+                nc.sync.dma_start(
+                    out=out_rows[g, :, i - 1 : i + 1, :], in_=result[g][:, i - 1 : i + 1, :]
+                )
+            if t + TILES < GROUPS * TILES:
+                for c in range(PASSES):
+                    multiply(t + TILES, c)

@@ -26,6 +26,7 @@ UNIT = PACK * N_TILE
 RUN = 4
 CHUNKS = ((0, 2), (2, 5))
 VECTOR_GROUPS = (0, 3, 4)
+ALONE = (0, 1, 18, 19)
 
 
 def tile_unicorelinearfp4_kernel(tc, x, weight, wscales, bias, grad_out, out):
@@ -154,10 +155,11 @@ def tile_unicorelinearfp4_kernel(tc, x, weight, wscales, bias, grad_out, out):
                         g_q[(c, g)] = quantise(pair[c], E5M2, "g%d_%d" % (c, g))
             empty(t, 0, False)
             empty(t, 1, t // TILES in VECTOR_GROUPS)
-            if t % 2 == 1:
+            if t in ALONE or t % 2 == 1:
                 g, i = divmod(t, TILES)
+                i0 = i if t in ALONE else i - 1
                 nc.sync.dma_start(
-                    out=out_rows[g, :, i - 1 : i + 1, :], in_=result[g][:, i - 1 : i + 1, :]
+                    out=out_rows[g, :, i0 : i + 1, :], in_=result[g][:, i0 : i + 1, :]
                 )
             if t + TILES < GROUPS * TILES:
                 for c in range(PASSES):

@@ -25,7 +25,8 @@ GROUPS = N_FEAT // (TILES * P)
 UNIT = PACK * N_TILE
 RUN = 4
 CHUNKS = ((0, 2), (2, 5))
-VECTOR_GROUPS = (0, 3, 4)
+VECTOR_TILES = (1, 2, 3, 13, 14, 15, 16, 17, 18, 19)
+FIRST_UNITS = (4, 2)
 ALONE = (0, 1, 18, 19)
 
 
@@ -38,7 +39,7 @@ def tile_unicorelinearfp4_kernel(tc, x, weight, wscales, bias, grad_out, out):
 
     with ExitStack() as ctx:
         raw = ctx.enter_context(tc.tile_pool(name="raw", bufs=1))
-        stage = ctx.enter_context(tc.tile_pool(name="stage", bufs=6))
+        stage = ctx.enter_context(tc.tile_pool(name="stage", bufs=8))
         keep = ctx.enter_context(tc.tile_pool(name="keep", bufs=1))
         res = ctx.enter_context(tc.tile_pool(name="res", bufs=1))
         psum = ctx.enter_context(tc.psum_pool(name="psum", bufs=8))
@@ -72,28 +73,34 @@ def tile_unicorelinearfp4_kernel(tc, x, weight, wscales, bias, grad_out, out):
             )
             return grouped
 
-        def regroup_g(copy, c, g):
+        def regroup_g(copy, c, t0, count):
+            g, i0 = divmod(t0, TILES)
             chunk = [n for n, (g0, g1) in enumerate(CHUNKS) if g0 <= g < g1][0]
             first = (g - CHUNKS[chunk][0]) * N_TILE
             grouped = stage.tile([P, UNIT], BF16, name="grouped", align_bytes=64)
             copy(
-                out=grouped[:].rearrange("p (i w j) -> p w j i", i=TILES, j=PACK),
+                out=grouped[:, : count * P * PACK].rearrange("p (i w j) -> p w j i", i=count, j=PACK),
                 in_=g_raw[(chunk, c)][:, :, first : first + N_TILE].rearrange(
                     "p j (w i) -> p w j i", i=TILES
-                ),
+                )[:, :, :, i0 : i0 + count],
             )
             return grouped
 
-        def quantise(grouped, fmt, name):
-            codes = keep.tile([P, N_TILE], U32, name=name + "_codes", align_bytes=64)
-            scales = keep.tile([P, N_TILE], U8, name=name + "_scales", align_bytes=64)
-            nc.vector.quantize_mx(out=codes[:].bitcast(fmt), scales=scales[:], in_=grouped[:])
+        def quantise(grouped, fmt, name, words=N_TILE):
+            codes = keep.tile([P, words], U32, name=name + "_codes", align_bytes=64)
+            scales = keep.tile([P, words], U8, name=name + "_scales", align_bytes=64)
+            nc.vector.quantize_mx(
+                out=codes[:].bitcast(fmt), scales=scales[:], in_=grouped[:, : words * PACK]
+            )
             return codes, scales
 
+        def quantise_g(grouped, c, t0, count):
+            codes, scales = quantise(grouped, E5M2, "g%d_%d" % (c, t0), count * P)
+            for i in range(count):
+                g_q[(c, t0 + i)] = (codes, scales, slice(i * P, (i + 1) * P))
+
         def multiply(t, c):
-            g, i = divmod(t, TILES)
-            codes, scales = g_q[(c, g)]
-            cols = slice(i * P, (i + 1) * P)
+            codes, scales, cols = g_q[(c, t)]
             for h in range(HALVES):
                 if c == 0:
                     acc[(t, h)] = psum.tile([P, N_TILE], F32, name="acc")
@@ -139,22 +146,25 @@ def tile_unicorelinearfp4_kernel(tc, x, weight, wscales, bias, grad_out, out):
             second = regroup_x(nc.scalar.copy, c, 1)
             x_q[(c, 0)] = quantise(first, E4M3, "x%d_0" % c)
             x_q[(c, 1)] = quantise(second, E4M3, "x%d_1" % c)
-            first = regroup_g(nc.vector.tensor_copy, c, 0)
-            later[c] = regroup_g(nc.scalar.copy, c, 1)
-            g_q[(c, 0)] = quantise(first, E5M2, "g%d_0" % c)
-            for t in range(TILES):
-                multiply(t, c)
+            later[c] = regroup_g(nc.scalar.copy, c, TILES, TILES)
+            count = FIRST_UNITS[c]
+            for t0 in range(0, TILES, count):
+                quantise_g(regroup_g(nc.vector.tensor_copy, c, t0, count), c, t0, count)
+                for t in range(t0, t0 + count):
+                    multiply(t, c)
         for c in range(PASSES):
-            g_q[(c, 1)] = quantise(later[c], E5M2, "g%d_1" % c)
+            quantise_g(later[c], c, TILES, TILES)
 
         for t in range(GROUPS * TILES):
             if t == TILES:
                 for g in range(2, GROUPS):
-                    pair = [regroup_g(nc.vector.tensor_copy, c, g) for c in range(PASSES)]
+                    pair = [
+                        regroup_g(nc.vector.tensor_copy, c, g * TILES, TILES) for c in range(PASSES)
+                    ]
                     for c in range(PASSES):
-                        g_q[(c, g)] = quantise(pair[c], E5M2, "g%d_%d" % (c, g))
+                        quantise_g(pair[c], c, g * TILES, TILES)
             empty(t, 0, False)
-            empty(t, 1, t // TILES in VECTOR_GROUPS)
+            empty(t, 1, t in VECTOR_TILES)
             if t in ALONE or t % 2 == 1:
                 g, i = divmod(t, TILES)
                 i0 = i if t in ALONE else i - 1

@@ -43,7 +43,6 @@ def tile_unicorelinearfp4_kernel(tc, x, weight, wscales, bias, grad_out, out):
         keep = ctx.enter_context(tc.tile_pool(name="keep", bufs=1))
         res = ctx.enter_context(tc.tile_pool(name="res", bufs=1))
         psum = ctx.enter_context(tc.psum_pool(name="psum", bufs=8))
-        ctx.enter_context(tc.manual_schedule())
 
         x_raw = {}
         g_raw = {}

from contextlib import ExitStack

import concourse.mybir as mybir

T_TOKENS, K_FEAT, N_FEAT = 1024, 1024, 2560
FLOPS = 2 * T_TOKENS * K_FEAT * N_FEAT
BYTES = 2 * (T_TOKENS * K_FEAT + T_TOKENS * N_FEAT + N_FEAT) + 4 * N_FEAT * K_FEAT

BF16 = mybir.dt.bfloat16
F32 = mybir.dt.float32
U32 = mybir.dt.uint32
U8 = mybir.dt.uint8
E4M3 = mybir.dt.float8_e4m3fn_x4
E5M2 = mybir.dt.float8_e5m2_x4
COPY = mybir.ActivationFunctionType.Copy
MULT = mybir.AluOpType.mult

P = 128
PACK = 4
PASSES = T_TOKENS // (P * PACK)
N_TILE = 512
HALVES = K_FEAT // N_TILE
TILES = 4
GROUPS = N_FEAT // (TILES * P)
UNIT = PACK * N_TILE
RUN = 4
CHUNKS = ((0, 2), (2, 5))
VECTOR_TILES = (1, 2, 3, 13, 14, 15, 16, 17, 18, 19)
FIRST_UNITS = (4, 2)
ALONE = (0, 1, 18, 19)


def tile_unicorelinearfp4_kernel(tc, x, weight, wscales, bias, grad_out, out):
    nc = tc.nc
    x_rows = x.flatten_outer_dims().rearrange("(c p j) k -> c p j k", c=PASSES, p=P, j=PACK)
    g_rows = grad_out.flatten_outer_dims().rearrange("(c p j) n -> c p j n", c=PASSES, p=P, j=PACK)
    out_rows = out.rearrange("(g p i) k -> g p i k", p=P, i=TILES)
    ws_cols = wscales.rearrange("(g p i) o -> p g (i o)", p=P, i=TILES)

    with ExitStack() as ctx:
        raw = ctx.enter_context(tc.tile_pool(name="raw", bufs=1))
        stage = ctx.enter_context(tc.tile_pool(name="stage", bufs=8))
        keep = ctx.enter_context(tc.tile_pool(name="keep", bufs=1))
        res = ctx.enter_context(tc.tile_pool(name="res", bufs=1))
        psum = ctx.enter_context(tc.psum_pool(name="psum", bufs=8))

        x_raw = {}
        g_raw = {}
        x_q = {}
        g_q = {}
        acc = {}

        def load_x(c):
            x_raw[c] = raw.tile([P, PACK, K_FEAT], BF16, name="x_raw%d" % c)
            nc.sync.dma_start(out=x_raw[c][:], in_=x_rows[c, :, :, :])

        def load_g(chunk, c):
            g0, g1 = CHUNKS[chunk]
            width = (g1 - g0) * N_TILE
            g_raw[(chunk, c)] = raw.tile([P, PACK, width], BF16, name="g_raw%d_%d" % (chunk, c))
            nc.sync.dma_start(
                out=g_raw[(chunk, c)][:], in_=g_rows[c, :, :, g0 * N_TILE : g1 * N_TILE]
            )

        def regroup_x(copy, c, h):
            grouped = stage.tile([P, UNIT], BF16, name="grouped", align_bytes=64)
            copy(
                out=grouped[:].rearrange("p (w i j) -> p w j i", i=RUN, j=PACK),
                in_=x_raw[c][:, :, h * N_TILE : (h + 1) * N_TILE].rearrange(
                    "p j (w i) -> p w j i", i=RUN
                ),
            )
            return grouped

        def regroup_g(copy, c, t0, count):
            g, i0 = divmod(t0, TILES)
            chunk = [n for n, (g0, g1) in enumerate(CHUNKS) if g0 <= g < g1][0]
            first = (g - CHUNKS[chunk][0]) * N_TILE
            grouped = stage.tile([P, UNIT], BF16, name="grouped", align_bytes=64)
            copy(
                out=grouped[:, : count * P * PACK].rearrange("p (i w j) -> p w j i", i=count, j=PACK),
                in_=g_raw[(chunk, c)][:, :, first : first + N_TILE].rearrange(
                    "p j (w i) -> p w j i", i=TILES
                )[:, :, :, i0 : i0 + count],
            )
            return grouped

        def quantise(grouped, fmt, name, words=N_TILE):
            codes = keep.tile([P, words], U32, name=name + "_codes", align_bytes=64)
            scales = keep.tile([P, words], U8, name=name + "_scales", align_bytes=64)
            nc.vector.quantize_mx(
                out=codes[:].bitcast(fmt), scales=scales[:], in_=grouped[:, : words * PACK]
            )
            return codes, scales

        def quantise_g(grouped, c, t0, count):
            codes, scales = quantise(grouped, E5M2, "g%d_%d" % (c, t0), count * P)
            for i in range(count):
                g_q[(c, t0 + i)] = (codes, scales, slice(i * P, (i + 1) * P))

        def multiply(t, c):
            codes, scales, cols = g_q[(c, t)]
            for h in range(HALVES):
                if c == 0:
                    acc[(t, h)] = psum.tile([P, N_TILE], F32, name="acc")
                x_codes, x_scales = x_q[(c, h)]
                nc.tensor.matmul_mx(
                    out=acc[(t, h)][:],
                    lhsT=codes[:, cols].bitcast(E5M2),
                    lhsT_scale=scales[:, cols],
                    rhs=x_codes[:].bitcast(E4M3),
                    rhs_scale=x_scales[:],
                    start=(c == 0),
                    stop=(c == PASSES - 1),
                )

        def empty(t, h, on_vector):
            g, i = divmod(t, TILES)
            dst = result[g][:, i, h * N_TILE : (h + 1) * N_TILE]
            if on_vector:
                nc.vector.tensor_scalar(
                    out=dst, in0=acc[(t, h)][:], scalar1=ws[:, t : t + 1], scalar2=None, op0=MULT
                )
            else:
                nc.scalar.activation(out=dst, in_=acc[(t, h)][:], func=COPY, scale=ws[:, t : t + 1])

        load_x(0)
        load_g(0, 0)
        load_x(1)
        load_g(0, 1)
        load_g(1, 0)
        load_g(1, 1)

        ws_bf = keep.tile([P, GROUPS, TILES], BF16, name="ws_bf")
        ws = keep.tile([P, GROUPS * TILES], F32, name="ws")
        with nc.allow_non_contiguous_dma(reason="wscales: 4 neighbouring rows of out a partition"):
            nc.scalar.dma_start(out=ws_bf[:], in_=ws_cols)
        nc.scalar.activation(out=ws[:], in_=ws_bf[:].rearrange("p g i -> p (g i)"), func=COPY)

        result = [res.tile([P, TILES, K_FEAT], F32, name="result%d" % g) for g in range(GROUPS)]

        later = {}
        for c in range(PASSES):
            first = regroup_x(nc.vector.tensor_copy, c, 0)
            second = regroup_x(nc.scalar.copy, c, 1)
            x_q[(c, 0)] = quantise(first, E4M3, "x%d_0" % c)
            x_q[(c, 1)] = quantise(second, E4M3, "x%d_1" % c)
            later[c] = regroup_g(nc.scalar.copy, c, TILES, TILES)
            count = FIRST_UNITS[c]
            for t0 in range(0, TILES, count):
                quantise_g(regroup_g(nc.vector.tensor_copy, c, t0, count), c, t0, count)
                for t in range(t0, t0 + count):
                    multiply(t, c)
        for c in range(PASSES):
            quantise_g(later[c], c, TILES, TILES)

        for t in range(GROUPS * TILES):
            if t == TILES:
                for g in range(2, GROUPS):
                    pair = [
                        regroup_g(nc.vector.tensor_copy, c, g * TILES, TILES) for c in range(PASSES)
                    ]
                    for c in range(PASSES):
                        quantise_g(pair[c], c, g * TILES, TILES)
            empty(t, 0, False)
            empty(t, 1, t in VECTOR_TILES)
            if t in ALONE or t % 2 == 1:
                g, i = divmod(t, TILES)
                i0 = i if t in ALONE else i - 1
                nc.sync.dma_start(
                    out=out_rows[g, :, i0 : i + 1, :], in_=result[g][:, i0 : i + 1, :]
                )
            if t + TILES < GROUPS * TILES:
                for c in range(PASSES):
                    multiply(t + TILES, c)
